import numpy as np
import ml_dtypes


def mxq(x, axis, fmt="e4m3"):
    dtype, down = {"e4m3": (ml_dtypes.float8_e4m3fn, 7), "e5m2": (ml_dtypes.float8_e5m2, 14)}[fmt]
    v = np.moveaxis(np.asarray(x, np.float32).astype(ml_dtypes.bfloat16).astype(np.float64), axis, -1)
    blocks = v.reshape(v.shape[:-1] + (-1, 32))
    amax = np.abs(blocks).max(-1, keepdims=True)
    byte = np.maximum(np.where(amax > 0, np.frexp(amax)[1] - 1 + 127, 0) - down, 1)
    scale = np.exp2(byte - 127.0)
    codes = (blocks / scale).astype(np.float32).astype(dtype).astype(np.float64)
    return np.moveaxis((codes * scale).reshape(v.shape), -1, axis)


WIDE = False


def mx_kscale(k):
    if not WIDE:
        return np.ones(k)
    levels = np.array([30, -30])
    if k % 512:
        return np.exp2(np.random.permutation(np.resize(levels, k // 32))).repeat(32)
    a = np.empty((k // 512, 16))
    for p in range(k // 512):
        a[p, :8] = np.random.permutation(np.resize(levels, 8))
        for g in range(8):
            far = levels[np.abs(levels - a[p, g]) >= 10]
            a[p, g + 8] = far[np.random.randint(len(far))]
    return np.exp2(a.ravel()).repeat(32)


BF16 = ml_dtypes.bfloat16


def bf(x):
    return np.asarray(x, np.float32).astype(BF16)


def f64(x):
    return np.asarray(x).astype(np.float64)


E2M1 = np.array([0.0, 0.5, 1.0, 1.5, 2.0, 3.0, 4.0, 6.0, -0.0, -0.5, -1.0, -1.5, -2.0, -3.0, -4.0, -6.0])


def pack_weight(w, fmt):
    k, n = w.shape
    w = f64(bf(w)).reshape(k // 32, 32, n)
    amax = np.abs(w).max(1)
    if fmt == "e4m3":
        byte = np.frexp(amax)[1] - 1 + 127 - 7
    else:
        mant, ex = np.frexp(amax / 6.0)
        byte = np.where(mant > 0.5, ex, ex - 1) + 127
    byte = np.clip(np.where(amax > 0, byte, 1), 1, 254)
    scaled = (w * np.exp2(127.0 - byte)[:, None, :]).reshape(k, n).astype(np.float32)
    by_word = np.ascontiguousarray(scaled.reshape(k // 512, 128, 4, n).transpose(0, 1, 3, 2))
    if fmt == "e4m3":
        words = by_word.astype(ml_dtypes.float8_e4m3fn).view(np.uint8)
    else:
        c = by_word.astype(ml_dtypes.float4_e2m1fn).view(np.uint8) & 0xF
        words = c[..., 0::2] | (c[..., 1::2] << 4)
    return np.ascontiguousarray(words), np.ascontiguousarray(byte.astype(np.uint8).reshape(k // 512, 16, n))


def unpack_weight(words, scales, fmt):
    g, p, n, _ = words.shape
    if fmt == "e4m3":
        vals = np.ascontiguousarray(words).view(ml_dtypes.float8_e4m3fn).astype(np.float64)
    else:
        nib = np.empty((g, p, n, 4), np.uint8)
        nib[..., 0::2] = words & 0xF
        nib[..., 1::2] = words >> 4
        vals = E2M1[nib]
    vals = vals * np.repeat(np.exp2(scales.astype(np.float64) - 127.0), 8, axis=1)[..., None]
    return vals.transpose(0, 1, 3, 2).reshape(g * 512, n)

def pack4(w):
    words, scales = pack_weight(w, "e2m1")
    return words.reshape(words.shape[0], 128, -1), scales


def unpack4(words, scales):
    return unpack_weight(words.reshape(words.shape[0], 128, -1, 2), scales, "e2m1")


B, N, D, H, NS, SK1, SK2 = 1, 2048, 1024, 16, 10, 512, 1024
HD = D // H
D4 = np.array([0.4829629131445341, 0.8365163037378079, 0.2241438680420134, -0.1294095225512604])
TAPS = len(D4)
SPARSE_DILATIONS = (SK1, SK2)


def softmax(v, axis):
    e = np.exp(v - v.max(axis, keepdims=True))
    return e / e.sum(axis, keepdims=True)


def sigmoid(v):
    return 1.0 / (1.0 + np.exp(-v))


def shift_right(t, s):
    if s == 0:
        return t
    return np.pad(t, ((0, 0), (0, 0), (s, 0), (0, 0)))[:, :, :N, :]


def to_heads(t):
    return t.reshape(B, N, H, HD).transpose(0, 2, 1, 3)


def setup_inputs():
    s = mx_kscale(D)
    x = bf(np.random.standard_normal((B, N, D)) * s)
    Wkv_words, Wkv_scales = pack4(np.random.standard_normal((D, D + D)) * D ** -0.5 / s[:, None])
    return {"x": x,
            "Wkv_words": Wkv_words,
            "Wkv_scales": Wkv_scales,
            "bkv": bf(np.random.standard_normal(D + D) * 0.2),
            "scale_gain": bf(np.random.standard_normal((NS, H)) * 0.5),
            "skip_w": bf(-1.0 + np.random.standard_normal(len(SPARSE_DILATIONS)) * 0.3)}


def reference(x, Wkv_words, Wkv_scales, bkv, scale_gain, skip_w):
    kv = (mxq(f64(x), 2, "e5m2") @ unpack4(Wkv_words, Wkv_scales)) + f64(bkv)
    k, v = to_heads(kv[..., :D]), to_heads(kv[..., D:])
    k_mag = np.sqrt((k * k).sum(-1, keepdims=True))
    field = v * k_mag
    gains = softmax(f64(scale_gain), 0)
    acc = np.zeros_like(field)
    for j in range(NS):
        d = 1 << j
        y = sum(D4[t] * shift_right(field, (TAPS - 1 - t) * d) for t in range(TAPS))
        acc = acc + gains[j][None, :, None, None] * y
    field = acc
    sw = sigmoid(f64(skip_w))
    skip = sum(sw[i] * shift_right(field, d) for i, d in enumerate(SPARSE_DILATIONS))
    return field + skip

@@ -1,0 +1,450 @@
+from contextlib import ExitStack
+
+import concourse.mybir as mybir
+from concourse.masks import make_identity
+
+N, D, H, HD, NS = 2048, 1024, 16, 64, 10
+D4 = (0.4829629131445341, 0.8365163037378079, 0.2241438680420134, -0.1294095225512604)
+FLOPS = 2 * N * D * 2 * D
+
+F32 = mybir.dt.float32
+BF16 = mybir.dt.bfloat16
+I32 = mybir.dt.int32
+U32 = mybir.dt.uint32
+U8 = mybir.dt.uint8
+E5M2X4 = mybir.dt.float8_e5m2_x4
+E2M1X4 = mybir.dt.float4_e2m1fn_x4
+ALU = mybir.AluOpType
+ACT = mybir.ActivationFunctionType
+AX = mybir.AxisListType
+
+P = 128
+R = 8
+HALVES = 2
+PASSES = 2
+RC = 4
+TILES = 8
+HALO = 2
+LEAD = 128
+ROW = LEAD + 2 * P
+PITCH = H * ROW + 8
+CHAINS = ((1, 1, 1, 1, 1, 1, 2, 2), (2, 2, 2, 2, 2, 2, 2, 3))
+
+
+def tile_causalwaveletfieldattentionh_pa_kernel(tc, x, Wkv_words, Wkv_scales, bkv, scale_gain, skip_w, out):
+    nc = tc.nc
+    with ExitStack() as ctx:
+        keep = ctx.enter_context(tc.tile_pool(name="keep", bufs=1))
+        work = ctx.enter_context(tc.tile_pool(name="work", bufs=2))
+        psum = ctx.enter_context(tc.psum_pool(name="psum", bufs=1))
+
+        ctx.enter_context(tc.manual_schedule())
+
+        def bank():
+            return psum.tile([P, 512], F32, name="bank", tag="bank", bufs=7)
+
+        plane = keep.tile([P, PASSES, 2 * D], U8, name="plane", align_bytes=64)
+        nc.vector.memset(plane[:].rearrange("p g n -> p (g n)").bitcast(I32), 0)
+        bk_rows = keep.tile([P, P], BF16, name="bk_rows")
+        nc.vector.memset(bk_rows[:], 0.0)
+        ident = keep.tile([P, P], F32, name="ident")
+        make_identity(nc, ident[:])
+        filt = keep.tile([P, H, ROW], F32, name="filt", tag="field1")
+        for q in range(4):
+            nc.gpsimd.memset(filt[:, 4 * q:4 * (q + 1), :], 0.0)
+
+        half = keep.tile([P, RC * H], F32, name="half")
+        nc.gpsimd.memset(half[:], 0.5)
+
+        x_rows = {}
+
+        def load_x(a, r):
+            xs = work.tile([P, D], BF16, name="xs", tag="ksq", bufs=7)
+            nc.sync.dma_start(out=xs[:], in_=x[0, 1024 * a:1024 * (a + 1), :].rearrange("(p r) k -> p r k", r=R)[:, r, :])
+            x_rows[a, r] = xs[:]
+
+        def load_x_pair(a, r):
+            xs = work.tile([P, 2, D], BF16, name="xs2", tag="near1", bufs=3)
+            nc.sync.dma_start(out=xs[:], in_=x[0, 1024 * a:1024 * (a + 1), :].rearrange("(p r) k -> p r k", r=R)[:, r:r + 2, :])
+            x_rows[a, r], x_rows[a, r + 1] = xs[:, 0, :], xs[:, 1, :]
+
+        load_x(0, 0)
+        load_x(0, 1)
+        gain_raw = keep.tile([P, NS, H], BF16, name="gain_raw")
+        nc.sync.dma_start(out=gain_raw[:].rearrange("p j h -> p (j h)"),
+                          in_=scale_gain.rearrange("j h -> (j h)").partition_broadcast(P))
+        skip_raw = keep.tile([P, 2], BF16, name="skip_raw")
+        nc.sync.dma_start(out=skip_raw[:], in_=skip_w.partition_broadcast(P))
+        nc.sync.dma_start(out=bk_rows[0:TILES, :].rearrange("t (h i) -> t h i", i=8),
+                          in_=bkv[0:D].rearrange("(h t i) -> t h i", t=TILES, i=8))
+        load_x(0, 2)
+        load_x(0, 3)
+        for q in range(4):
+            nc.sync.dma_start(out=plane[32 * q:32 * q + 4, :, :].bitcast(I32),
+                              in_=Wkv_scales[:, 4 * q:4 * q + 4, :].rearrange("g r n -> r g n").bitcast(I32))
+        wk_raw = work.tile([P, PASSES, 2 * D], U8, name="wk_raw", tag="stage", bufs=3)
+        nc.sync.dma_start(out=wk_raw[:].bitcast(I32),
+                          in_=Wkv_words[:, :, 0:2 * D].rearrange("g p n -> p g n").bitcast(I32))
+        load_x_pair(0, 4)
+        load_x_pair(0, 6)
+        wv = keep.tile([P, PASSES, 2 * D], U8, name="wv", align_bytes=64)
+        nc.sync.dma_start(out=wv[:].bitcast(I32),
+                          in_=Wkv_words[:, :, 2 * D:4 * D].rearrange("g p n -> p g n").bitcast(I32))
+        bv = keep.tile([P, D], BF16, name="bv")
+        nc.sync.dma_start(out=bv[:], in_=bkv[D:2 * D].partition_broadcast(P))
+        load_x_pair(1, 0)
+
+        wk = keep.tile([P, PASSES, 2 * D], U8, name="wk", align_bytes=64)
+        sk = keep.tile([P, PASSES, D], U8, name="sk", align_bytes=64)
+        bk_f32 = keep.tile([P, P], F32, name="bk_f32")
+        bk = keep.tile([P, TILES], F32, name="bk")
+        top = keep.tile([P, H], F32, name="top")
+        gain = keep.tile([P, NS, H], F32, name="gain")
+        sw = keep.tile([P, 2], F32, name="sw")
+        total = keep.tile([P, H], F32, name="total")
+        coef = keep.tile([P, 2 * NS + 1, H], F32, name="coef")
+        coef_ch = keep.tile([P, 2 * NS + 1, TILES], F32, name="coef_ch")
+        def order_key_columns():
+            for g in range(PASSES):
+                nc.vector.tensor_copy(out=sk[:, g, :].bitcast(I32).rearrange("p (t h w) -> p t h w", t=TILES, h=H),
+                                      in_=plane[:, g, 0:D].bitcast(I32).rearrange("p (h t w) -> p t h w", t=TILES, h=H))
+            for g in range(PASSES):
+                nc.scalar.copy(out=wk[:, g, :].bitcast(U32).rearrange("p (t h w) -> p t h w", t=TILES, h=H),
+                               in_=wk_raw[:, g, :].bitcast(U32).rearrange("p (h t w) -> p t h w", t=TILES, h=H))
+
+        nc.vector.tensor_copy(out=bk_f32[:], in_=bk_rows[:])
+
+        def key_bias():
+            bk_ps = bank()
+            nc.tensor.transpose(bk_ps[:, 0:P], bk_f32[:], ident[:])
+            nc.vector.tensor_copy(out=bk[:], in_=bk_ps[:, 0:TILES])
+
+        def coefficients():
+            nc.vector.tensor_reduce(out=top[:], in_=gain_raw[:].rearrange("p j h -> p h j"), axis=AX.X, op=ALU.max)
+            nc.vector.tensor_tensor(out=gain[:], in0=gain_raw[:], in1=top[:].unsqueeze(1).to_broadcast([P, NS, H]), op=ALU.subtract)
+
+        def coefficients_rest():
+            nc.scalar.activation(out=gain[:], in_=gain[:], func=ACT.Exp)
+            nc.scalar.activation(out=sw[:], in_=skip_raw[:], func=ACT.Tanh, scale=0.5)
+            nc.vector.tensor_reduce(out=total[:], in_=gain[:].rearrange("p j h -> p h j"), axis=AX.X, op=ALU.add)
+            nc.vector.tensor_scalar(out=sw[:], in0=sw[:], scalar1=0.5, scalar2=0.5, op0=ALU.mult, op1=ALU.add)
+            nc.vector.reciprocal(out=total[:], in_=total[:])
+            nc.vector.tensor_tensor(out=gain[:], in0=gain[:], in1=total[:].unsqueeze(1).to_broadcast([P, NS, H]), op=ALU.mult)
+            nc.vector.tensor_scalar(out=coef[:, 0:NS, :], in0=gain[:], scalar1=D4[2], scalar2=None, op0=ALU.mult)
+            nc.vector.tensor_scalar(out=coef[:, NS, :], in0=gain[:, NS - 1, :], scalar1=D4[1], scalar2=None, op0=ALU.mult)
+            nc.vector.tensor_scalar(out=coef[:, NS + 1:, :], in0=gain[:], scalar1=D4[0], scalar2=None, op0=ALU.mult)
+            nc.vector.scalar_tensor_tensor(out=coef[:, 1:NS, :], in0=gain[:, 0:NS - 1, :], scalar=D4[1], in1=coef[:, 1:NS, :],
+                                           op0=ALU.mult, op1=ALU.add)
+            nc.vector.tensor_reduce(out=top[:], in_=gain[:].rearrange("p j h -> p h j"), axis=AX.X, op=ALU.add)
+            for hh in range(2):
+                rows = slice(HD * hh, HD * (hh + 1))
+                nc.vector.tensor_copy(out=coef_ch[rows], in_=coef[rows].rearrange("p s (j e) -> p s j e", e=2)[:, :, :, hh])
+
+        toep = keep.tile([P, H, 2 * P], F32, name="toep")
+
+        def build_filter():
+            nc.gpsimd.tensor_scalar(out=filt[:, :, LEAD], in0=top[:], scalar1=D4[3], scalar2=0.0, op0=ALU.mult, op1=ALU.add)
+            for k in range(3, NS + 1):
+                nc.gpsimd.tensor_copy(out=filt[:, :, LEAD + 2 ** (k - 3)], in_=coef[:, k, :])
+            for j in range(3, NS):
+                nc.gpsimd.tensor_copy(out=filt[:, :, LEAD + 3 * 2 ** (j - 3)], in_=coef[:, NS + 1 + j, :])
+
+        def skip_filter():
+            used = (slice(0, 49), slice(0, 33, 32), slice(0, 1))
+            for dst, src, i in ((3, 2, 0), (3, 1, 1), (2, 1, 0), (2, 0, 1), (1, 0, 0)):
+                to = filt[:, :, LEAD + 64 * dst:LEAD + 64 * (dst + 1)][:, :, used[src]]
+                nc.vector.scalar_tensor_tensor(out=to, in0=filt[:, :, LEAD + 64 * src:LEAD + 64 * (src + 1)][:, :, used[src]],
+                                               scalar=sw[:, i:i + 1], in1=to, op0=ALU.mult, op1=ALU.add)
+
+        flat = out.rearrange("b h n c -> (b h n c)")
+
+        def park_filter():
+            nc.sync.dma_start(out=flat[0:P * PITCH].rearrange("(p w) -> p w", w=PITCH)[:, 0:H * ROW],
+                              in_=filt[:].rearrange("p h w -> p (h w)"))
+
+        def fetch_filter():
+            skew = flat[0:P * (PITCH - 1)].rearrange("(p w) -> p w", w=PITCH - 1)[:, 0:H * ROW]
+            nc.sync.dma_start(out=toep[:], in_=skew.rearrange("p (h w) -> p h w", w=ROW)[:, :, LEAD:])
+
+        field = {}
+        mag = keep.tile([P, HALVES, R, H], F32, name="mag")
+        grouped, codes, scales, ksq, ksum = {}, {}, {}, {}, {}
+
+        def turn_x(c, rr):
+            a, r = c // 2, RC * (c % 2) + rr
+            if rr == 0:
+                grouped[c] = work.tile([P, PASSES, RC, P, 2], F32, name="grouped", tag="grouped", align_bytes=64)
+            words = x_rows[a, r].bitcast(F32)
+            ps = bank()
+            for g in range(PASSES):
+                for u in range(2):
+                    nc.tensor.transpose(ps[:, (2 * g + u) * P:(2 * g + u + 1) * P],
+                                        words[:, 256 * g + u:256 * (g + 1):2], ident[:])
+            move = nc.vector.tensor_copy if (c == 1 or (c == 0 and rr % 2 == 1)) else nc.scalar.copy
+            move(out=grouped[c][:, :, rr, :, :], in_=ps[:].rearrange("k (g u p) -> k g p u", g=PASSES, u=2))
+
+        def quantize(c):
+            codes[c] = work.tile([P, PASSES, RC * P], U32, name="codes", tag="codes", bufs=3, align_bytes=64)
+            scales[c] = work.tile([P, PASSES, RC * P], U8, name="scales", tag="scales", bufs=3, align_bytes=64)
+            for g in range(PASSES):
+                nc.vector.quantize_mx(out=codes[c][:, g, :].bitcast(E5M2X4), scales=scales[c][:, g, :],
+                                      in_=grouped[c][:, g].rearrange("k r p u -> k (r p u)").bitcast(BF16))
+
+        def keys(c, t):
+            ps = bank()
+            for g in range(PASSES):
+                nc.tensor.matmul_mx(out=ps[:], lhsT=wk[:, g, 2 * P * t:2 * P * (t + 1)].bitcast(E2M1X4),
+                                    lhsT_scale=sk[:, g, P * t:P * (t + 1)],
+                                    rhs=codes[c][:, g, :].bitcast(E5M2X4), rhs_scale=scales[c][:, g, :],
+                                    start=(g == 0), stop=(g == PASSES - 1))
+            ksq[c, t] = work.tile([P, RC * P], F32, name="ksq", tag="ksq", bufs=7)
+            nc.scalar.activation(out=ksq[c, t][:], in_=ps[:], func=ACT.Square, bias=bk[:, t:t + 1])
+
+        def add_keys(c, t):
+            nc.vector.tensor_tensor(out=ksq[c, t % 2][:], in0=ksq[c, t % 2][:], in1=ksq[c, t][:], op=ALU.add)
+
+        def sum_keys(c, t):
+            if t == 0:
+                ksum[c] = psum.tile([P, RC * P], F32, name="ksum", tag="ksum", bufs=1)
+            for rr in range(RC):
+                nc.tensor.matmul(ksum[c][:, P * rr:P * (rr + 1)], lhsT=ksq[c, t][:, P * rr:P * (rr + 1)], rhs=ident[:],
+                                 is_transpose=True, start=(t == 0 and rr == 0), stop=(t == TILES - 1 and rr == RC - 1))
+
+        def magnitude(c):
+            to = mag[:, c // 2, RC * (c % 2):RC * (c % 2 + 1), :].rearrange("p r h -> p (r h)")
+            nc.vector.tensor_reduce(out=to, in_=ksum[c][:].rearrange("p (e i) -> p e i", i=8), axis=AX.X, op=ALU.add)
+            nc.gpsimd.tensor_tensor(out=to, in0=to, in1=half[:], op=ALU.pow)
+
+        raw_values = {}
+
+        def unit_view(u):
+            a, q, b = u // 8, u // 2 % 4, u % 2
+            if a not in field:
+                field[a] = keep.tile([P, R, D], F32, name="field", tag="field%d" % a)
+            return a, q, b
+
+        def values(u, e):
+            a, q, b = unit_view(u)
+            c = 2 * a + b
+            ps = raw_values[u, e] = bank()
+            for rr in (2 * e, 2 * e + 1):
+                for g in range(PASSES):
+                    nc.tensor.matmul_mx(out=ps[:, 256 * (rr % 2):256 * (rr % 2 + 1)],
+                                        lhsT=codes[c][:, g, P * rr:P * (rr + 1)].bitcast(E5M2X4),
+                                        lhsT_scale=scales[c][:, g, P * rr:P * (rr + 1)],
+                                        rhs=wv[:, g, 512 * q:512 * (q + 1)].bitcast(E2M1X4),
+                                        rhs_scale=plane[:, g, D + 256 * q:D + 256 * (q + 1)],
+                                        start=(g == 0), stop=(g == PASSES - 1))
+
+        def value_bias(u, e):
+            a, q, b = unit_view(u)
+            r0, cols = RC * b + 2 * e, slice(256 * q, 256 * (q + 1))
+            nc.vector.tensor_tensor(out=field[a][:, r0:r0 + 2, cols], in0=raw_values[u, e][:].rearrange("p (r c) -> p r c", r=2),
+                                    in1=bv[:, cols].unsqueeze(1).to_broadcast([P, 2, 256]), op=ALU.add)
+
+        def scale_values(u, e):
+            a, q, b = unit_view(u)
+            r0 = RC * b + 2 * e
+            if u == 1 and e == 1:
+                v = field[a][:, r0:r0 + 2, 256 * q:256 * (q + 1)].rearrange("p r (h c) -> p r h c", c=HD)
+                nc.vector.tensor_tensor(out=v, in0=v, op=ALU.mult,
+                                        in1=mag[:, a, r0:r0 + 2, 4 * q:4 * q + 4].unsqueeze(3).to_broadcast([P, 2, 4, HD]))
+            else:
+                for r in (r0, r0 + 1):
+                    for h in range(4 * q, 4 * q + 4):
+                        v = field[a][:, r, HD * h:HD * (h + 1)]
+                        nc.scalar.activation(out=v, in_=v, func=ACT.Copy, scale=mag[:, a, r, h:h + 1])
+
+        def run(calls):
+            for call in calls:
+                call[0](*call[1:])
+
+        first = keep.tile([P, TILES, R, HALO + P], F32, name="first")
+        second_raw = keep.tile([P, TILES, R, 64], F32, name="second_raw")
+        nc.vector.memset(first[:, :, :, 0:HALO].rearrange("p j r w -> p (j r) w"), 0.0)
+        skipped, sums = {}, {}
+
+        turned = {}
+
+        def turn_field(a, j):
+            ps = [bank(), bank()]
+            for r in range(R):
+                nc.tensor.transpose(ps[r // RC][:, P * (r % RC):P * (r % RC + 1)], field[a][:, r, P * j:P * (j + 1)], ident[:])
+            turned[a, j] = [b[:].rearrange("c (r p) -> c r p", p=P) for b in ps]
+
+        def add_skips(a, j):
+            views = turned[a, j]
+            q0 = first[:, j, :, HALO:HALO + 64]
+            q1 = second_raw[:, j]
+            if a == 0:
+                for b in range(2):
+                    rs = slice(RC * b, RC * (b + 1))
+                    nc.scalar.copy(out=q0[:, rs, :], in_=views[b][:, :, 0:64])
+                    nc.scalar.copy(out=q1[:, rs, :], in_=views[b][:, :, 64:P])
+                nc.vector.scalar_tensor_tensor(out=first[:, j, :, HALO + 64:], in0=q0, scalar=sw[:, 0:1], in1=q1,
+                                               op0=ALU.mult, op1=ALU.add)
+                skipped[a, j] = first[:, j]
+            else:
+                later = work.tile([P, R, HALO + P], F32, name="later", tag="grouped", align_bytes=64)
+                lo, hi = later[:, :, HALO:HALO + 64], later[:, :, HALO + 64:]
+                nc.scalar.copy(out=later[:, :, 0:HALO], in_=first[:, j, :, P:P + HALO])
+                for b in range(2):
+                    rs = slice(RC * b, RC * (b + 1))
+                    nc.vector.scalar_tensor_tensor(out=hi[:, rs, :], in0=q1[:, rs, :], scalar=sw[:, 1:2], in1=views[b][:, :, 64:P],
+                                                   op0=ALU.mult, op1=ALU.add)
+                    nc.vector.scalar_tensor_tensor(out=lo[:, rs, :], in0=q1[:, rs, :], scalar=sw[:, 0:1], in1=views[b][:, :, 0:64],
+                                                   op0=ALU.mult, op1=ALU.add)
+                for b in range(2):
+                    rs = slice(RC * b, RC * (b + 1))
+                    nc.vector.scalar_tensor_tensor(out=hi[:, rs, :], in0=views[b][:, :, 0:64], scalar=sw[:, 0:1], in1=hi[:, rs, :],
+                                                   op0=ALU.mult, op1=ALU.add)
+                nc.vector.scalar_tensor_tensor(out=lo, in0=q0, scalar=sw[:, 1:2], in1=lo, op0=ALU.mult, op1=ALU.add)
+                skipped[a, j] = later[:]
+
+        def tap_pieces(src, dst, shift):
+            whole, w = divmod(shift, R)
+            return ((dst[:, w:R, :], src[:, 0:R - w, HALO - whole:HALO - whole + P]),
+                    (dst[:, 0:w, :], src[:, R - w:R, HALO - whole - 1:HALO - whole - 1 + P]))
+
+        COEF_ROW = {1: 0, 2: 1, 4: 2, 3: NS + 1, 6: NS + 2, 12: NS + 3}
+
+        def start_sums(a, j):
+            starts = (1, 12, 6)[:CHAINS[a][j]]
+            sums[a, j] = []
+            for e, shift in enumerate(starts):
+                s = work.tile([P, R, P], F32, name="near", tag=("near0", "near1", "stage")[e], bufs=3)
+                for to, src in tap_pieces(skipped[a, j], s, shift):
+                    nc.scalar.activation(out=to, in_=src, func=ACT.Copy, scale=coef_ch[:, COEF_ROW[shift], j:j + 1])
+                sums[a, j].append(s)
+
+        def add_tap(a, j, e):
+            for shift in ((2, 3, 4, 12, 6), (2, 3, 4, 6), (2, 3, 4))[CHAINS[a][j] - 1][e:e + 1]:
+                for to, src in tap_pieces(skipped[a, j], sums[a, j][0], shift):
+                    nc.vector.scalar_tensor_tensor(out=to, in0=src, scalar=coef_ch[:, COEF_ROW[shift], j:j + 1], in1=to,
+                                                   op0=ALU.mult, op1=ALU.add)
+
+        acc = {}
+
+        def far_taps(a, j):
+            ps = acc[a, j] = [bank(), bank()]
+            for hh in range(2):
+                h = 2 * j + hh
+                for back in range(a + 1):
+                    for b in range(2):
+                        nc.tensor.matmul(ps[b][:].rearrange("p (r e c) -> p r e c", e=2, c=HD)[:, :, hh, :],
+                                         lhsT=toep[:, h, P * back:P * (back + 1)],
+                                         rhs=field[a - back][:, RC * b:RC * (b + 1), HD * h:HD * (h + 1)],
+                                         start=(hh == 0 and back == 0), stop=False)
+
+        def finish(a, j):
+            ps = acc[a, j]
+            last = len(sums[a, j]) - 1
+            for e, s in enumerate(reversed(sums[a, j])):
+                for r in range(R):
+                    nc.tensor.matmul(ps[r // RC][:, P * (r % RC):P * (r % RC + 1)], lhsT=s[:, r, :], rhs=ident[:],
+                                     is_transpose=True, start=False, stop=(e == last and r % RC == RC - 1))
+
+        def store(a, j):
+            ps = acc[a, j]
+            res = work.tile([P, 2, R, HD], F32, name="res", tag="stage", bufs=3)
+            for b in range(2):
+                nc.scalar.copy(out=res[:, :, RC * b:RC * (b + 1), :],
+                               in_=ps[b][:].rearrange("p (r e c) -> p e r c", e=2, c=HD))
+            nc.sync.dma_start(out=out[0, 2 * j:2 * j + 2, 1024 * a:1024 * (a + 1), :].rearrange("h (p r) c -> p h (r c)", r=R),
+                              in_=res[:].rearrange("p e r c -> p e (r c)"))
+
+        coefficients()
+        turn_x(0, 0)
+        turn_x(0, 1)
+        turn_x(0, 2)
+        turn_x(0, 3)
+        key_bias()
+        order_key_columns()
+        quantize(0)
+        coefficients_rest()
+        build_filter()
+        for rr in range(RC):
+            turn_x(1, rr)
+        load_x_pair(1, 2)
+        for c in range(2):
+            for t in range(TILES):
+                keys(c, t)
+                if c == 0 and t == 0:
+                    quantize(1)
+                if 2 <= t < TILES - 1:
+                    add_keys(c, t)
+                if c == 1 and t == 1:
+                    for tt in (0, 1, TILES - 1):
+                        sum_keys(0, tt)
+                    skip_filter()
+                    park_filter()
+                    magnitude(0)
+        fetch_filter()
+        values(0, 0)
+        values(0, 1)
+        for tt in (0, 1, TILES - 1):
+            sum_keys(1, tt)
+        values(1, 0)
+        values(1, 1)
+        value_bias(0, 0)
+        value_bias(0, 1)
+        magnitude(1)
+        scale_values(0, 0)
+        scale_values(0, 1)
+        value_bias(1, 0)
+        value_bias(1, 1)
+        scale_values(1, 0)
+        scale_values(1, 1)
+        values(2, 0)
+        values(2, 1)
+        key_work = [
+            ([], [(turn_x, 2, rr) for rr in range(RC)] + [(load_x_pair, 1, 6)], [(quantize, 2)]),
+            ([(keys, 2, t) for t in range(0, 4)], [(turn_x, 3, 0), (turn_x, 3, 1)], []),
+            ([(keys, 2, t) for t in range(4, 8)], [(sum_keys, 2, t) for t in range(0, 4)] + [(turn_x, 3, 2), (turn_x, 3, 3)], []),
+            ([(keys, 3, t) for t in range(0, 4)], [(sum_keys, 2, t) for t in range(4, 8)], [(quantize, 3), (magnitude, 2)]),
+            ([(keys, 3, t) for t in range(4, 8)], [(sum_keys, 3, t) for t in range(0, 4)], []),
+            ([], [(sum_keys, 3, t) for t in range(4, 8)], [(magnitude, 3)]),
+        ]
+        order = [(a, j) for a in range(HALVES) for j in range(TILES)]
+        turn_field(*order[0])
+        for e in range(2):
+            value_bias(2, e)
+        add_skips(*order[0])
+        start_sums(*order[0])
+        load_x_pair(1, 4)
+        for e in range(2):
+            scale_values(2, e)
+        for i, (a, j) in enumerate(order):
+            products, turns, after = key_work[i] if i < len(key_work) else ([], [], [])
+            more = i + 1 < len(order)
+            u = i + 3
+            if more:
+                turn_field(*order[i + 1])
+            if u < 16:
+                values(u, 0)
+                values(u, 1)
+            add_tap(a, j, 0)
+            if u < 16:
+                value_bias(u, 0)
+                value_bias(u, 1)
+            if more:
+                add_skips(*order[i + 1])
+            if u < 16:
+                scale_values(u, 0)
+                scale_values(u, 1)
+            if more:
+                start_sums(*order[i + 1])
+            if i > 0:
+                far_taps(*order[i - 1])
+                finish(*order[i - 1])
+                store(*order[i - 1])
+            add_tap(a, j, 1)
+            run(turns)
+            add_tap(a, j, 2)
+            run(after)
+            run(products)
+            add_tap(a, j, 3)
+            add_tap(a, j, 4)
+        far_taps(*order[-1])
+        finish(*order[-1])
+        store(*order[-1])

@@ -28,7 +28,8 @@ HALO = 2
 LEAD = 128
 ROW = LEAD + 2 * P
 PITCH = H * ROW + 8
-CHAINS = ((1, 1, 1, 1, 1, 1, 2, 2), (2, 2, 2, 2, 2, 2, 2, 3))
+EARLY_FROM = 15
+CHAINS = ((1, 1, 1, 1, 1, 2, 3, 3), (3, 2, 2, 2, 2, 2, 2, 2))
 
 
 def tile_causalwaveletfieldattentionh_pa_kernel(tc, x, Wkv_words, Wkv_scales, bkv, scale_gain, skip_w, out):
@@ -41,7 +42,7 @@ def tile_causalwaveletfieldattentionh_pa_kernel(tc, x, Wkv_words, Wkv_scales, bk
         ctx.enter_context(tc.manual_schedule())
 
         def bank():
-            return psum.tile([P, 512], F32, name="bank", tag="bank", bufs=7)
+            return psum.tile([P, 512], F32, name="bank", tag="bank", bufs=8)
 
         plane = keep.tile([P, PASSES, 2 * D], U8, name="plane", align_bytes=64)
         nc.vector.memset(plane[:].rearrange("p g n -> p (g n)").bitcast(I32), 0)
@@ -52,9 +53,6 @@ def tile_causalwaveletfieldattentionh_pa_kernel(tc, x, Wkv_words, Wkv_scales, bk
         filt = keep.tile([P, H, ROW], F32, name="filt", tag="field1")
         for q in range(4):
             nc.gpsimd.memset(filt[:, 4 * q:4 * (q + 1), :], 0.0)
-
-        half = keep.tile([P, RC * H], F32, name="half")
-        nc.gpsimd.memset(half[:], 0.5)
 
         x_rows = {}
 
@@ -205,15 +203,18 @@ def tile_causalwaveletfieldattentionh_pa_kernel(tc, x, Wkv_words, Wkv_scales, bk
 
         def sum_keys(c, t):
             if t == 0:
-                ksum[c] = psum.tile([P, RC * P], F32, name="ksum", tag="ksum", bufs=1)
+                ksum[c] = bank()
             for rr in range(RC):
                 nc.tensor.matmul(ksum[c][:, P * rr:P * (rr + 1)], lhsT=ksq[c, t][:, P * rr:P * (rr + 1)], rhs=ident[:],
                                  is_transpose=True, start=(t == 0 and rr == 0), stop=(t == TILES - 1 and rr == RC - 1))
 
-        def magnitude(c):
+        def square_sums(c):
             to = mag[:, c // 2, RC * (c % 2):RC * (c % 2 + 1), :].rearrange("p r h -> p (r h)")
             nc.vector.tensor_reduce(out=to, in_=ksum[c][:].rearrange("p (e i) -> p e i", i=8), axis=AX.X, op=ALU.add)
-            nc.gpsimd.tensor_tensor(out=to, in0=to, in1=half[:], op=ALU.pow)
+
+        def magnitude(c0, c1):
+            to = mag[:].rearrange("p a r h -> p (a r h)")[:, RC * H * c0:RC * H * (c1 + 1)]
+            nc.scalar.activation(out=to, in_=to, func=ACT.Sqrt)
 
         raw_values = {}
 
@@ -347,11 +348,12 @@ def tile_causalwaveletfieldattentionh_pa_kernel(tc, x, Wkv_words, Wkv_scales, bk
         def store(a, j):
             ps = acc[a, j]
             res = work.tile([P, 2, R, HD], F32, name="res", tag="stage", bufs=3)
+            rows = out[0, 2 * j:2 * j + 2, 1024 * a:1024 * (a + 1), :].rearrange("h (p r) c -> p h (r c)", r=R)
+            final = (a, j) == (HALVES - 1, TILES - 1)
             for b in range(2):
-                nc.scalar.copy(out=res[:, :, RC * b:RC * (b + 1), :],
-                               in_=ps[b][:].rearrange("p (r e c) -> p e r c", e=2, c=HD))
-            nc.sync.dma_start(out=out[0, 2 * j:2 * j + 2, 1024 * a:1024 * (a + 1), :].rearrange("h (p r) c -> p h (r c)", r=R),
-                              in_=res[:].rearrange("p e r c -> p e (r c)"))
+                move = nc.vector.tensor_copy if final and b == 1 else nc.scalar.copy
+                move(out=res[:, :, RC * b:RC * (b + 1), :], in_=ps[b][:].rearrange("p (r e c) -> p e r c", e=2, c=HD))
+            nc.sync.dma_start(out=rows, in_=res[:].rearrange("p e r c -> p e (r c)"))
 
         coefficients()
         turn_x(0, 0)
@@ -378,7 +380,7 @@ def tile_causalwaveletfieldattentionh_pa_kernel(tc, x, Wkv_words, Wkv_scales, bk
                         sum_keys(0, tt)
                     skip_filter()
                     park_filter()
-                    magnitude(0)
+                    square_sums(0)
         fetch_filter()
         values(0, 0)
         values(0, 1)
@@ -386,10 +388,12 @@ def tile_causalwaveletfieldattentionh_pa_kernel(tc, x, Wkv_words, Wkv_scales, bk
             sum_keys(1, tt)
         values(1, 0)
         values(1, 1)
+        magnitude(0, 0)
         value_bias(0, 0)
+        square_sums(1)
         value_bias(0, 1)
-        magnitude(1)
         scale_values(0, 0)
+        magnitude(1, 1)
         scale_values(0, 1)
         value_bias(1, 0)
         value_bias(1, 1)
@@ -401,9 +405,9 @@ def tile_causalwaveletfieldattentionh_pa_kernel(tc, x, Wkv_words, Wkv_scales, bk
             ([], [(turn_x, 2, rr) for rr in range(RC)] + [(load_x_pair, 1, 6)], [(quantize, 2)]),
             ([(keys, 2, t) for t in range(0, 4)], [(turn_x, 3, 0), (turn_x, 3, 1)], []),
             ([(keys, 2, t) for t in range(4, 8)], [(sum_keys, 2, t) for t in range(0, 4)] + [(turn_x, 3, 2), (turn_x, 3, 3)], []),
-            ([(keys, 3, t) for t in range(0, 4)], [(sum_keys, 2, t) for t in range(4, 8)], [(quantize, 3), (magnitude, 2)]),
+            ([(keys, 3, t) for t in range(0, 4)], [(sum_keys, 2, t) for t in range(4, 8)], [(quantize, 3), (square_sums, 2), (magnitude, 2, 2)]),
             ([(keys, 3, t) for t in range(4, 8)], [(sum_keys, 3, t) for t in range(0, 4)], []),
-            ([], [(sum_keys, 3, t) for t in range(4, 8)], [(magnitude, 3)]),
+            ([], [(sum_keys, 3, t) for t in range(4, 8)], [(square_sums, 3), (magnitude, 3, 3)]),
         ]
         order = [(a, j) for a in range(HALVES) for j in range(TILES)]
         turn_field(*order[0])
@@ -434,10 +438,13 @@ def tile_causalwaveletfieldattentionh_pa_kernel(tc, x, Wkv_words, Wkv_scales, bk
                 scale_values(u, 1)
             if more:
                 start_sums(*order[i + 1])
-            if i > 0:
+            if 0 < i <= EARLY_FROM:
                 far_taps(*order[i - 1])
+            if i > 0:
                 finish(*order[i - 1])
                 store(*order[i - 1])
+            if i >= EARLY_FROM:
+                far_taps(a, j)
             add_tap(a, j, 1)
             run(turns)
             add_tap(a, j, 2)
@@ -445,6 +452,5 @@ def tile_causalwaveletfieldattentionh_pa_kernel(tc, x, Wkv_words, Wkv_scales, bk
             run(products)
             add_tap(a, j, 3)
             add_tap(a, j, 4)
-        far_taps(*order[-1])
         finish(*order[-1])
         store(*order[-1])

@@ -24,11 +24,12 @@ HALVES = 2
 PASSES = 2
 RC = 4
 TILES = 8
-HALO = 2
+HALO = 4
 LEAD = 128
 ROW = LEAD + 2 * P
 PITCH = H * ROW + 8
 EARLY_FROM = 15
+ADDED = (4, 4)
 CHAINS = ((1, 1, 1, 1, 1, 2, 3, 3), (3, 2, 2, 2, 2, 2, 2, 2))
 
 
@@ -44,15 +45,19 @@ def tile_causalwaveletfieldattentionh_pa_kernel(tc, x, Wkv_words, Wkv_scales, bk
         def bank():
             return psum.tile([P, 512], F32, name="bank", tag="bank", bufs=8)
 
-        plane = keep.tile([P, PASSES, 2 * D], U8, name="plane", align_bytes=64)
-        nc.vector.memset(plane[:].rearrange("p g n -> p (g n)").bitcast(I32), 0)
         bk_rows = keep.tile([P, P], BF16, name="bk_rows")
         nc.vector.memset(bk_rows[:], 0.0)
+        plane = keep.tile([P, PASSES, 2 * D], U8, name="plane", align_bytes=64)
+        nc.vector.memset(plane[:].rearrange("p g n -> p (g n)").bitcast(I32), 0)
         ident = keep.tile([P, P], F32, name="ident")
         make_identity(nc, ident[:])
         filt = keep.tile([P, H, ROW], F32, name="filt", tag="field1")
+        nc.vector.memset(filt[:], 0.0)
+        nc.scalar.dma_start(out=bk_rows[0:TILES, :].rearrange("t (h i) -> t h i", i=8),
+                            in_=bkv[0:D].rearrange("(h t i) -> t h i", t=TILES, i=8))
         for q in range(4):
-            nc.gpsimd.memset(filt[:, 4 * q:4 * (q + 1), :], 0.0)
+            nc.scalar.dma_start(out=plane[32 * q:32 * q + 4, :, :].bitcast(I32),
+                                in_=Wkv_scales[:, 4 * q:4 * q + 4, :].rearrange("g r n -> r g n").bitcast(I32))
 
         x_rows = {}
 
@@ -66,25 +71,18 @@ def tile_causalwaveletfieldattentionh_pa_kernel(tc, x, Wkv_words, Wkv_scales, bk
             nc.sync.dma_start(out=xs[:], in_=x[0, 1024 * a:1024 * (a + 1), :].rearrange("(p r) k -> p r k", r=R)[:, r:r + 2, :])
             x_rows[a, r], x_rows[a, r + 1] = xs[:, 0, :], xs[:, 1, :]
 
-        load_x(0, 0)
-        load_x(0, 1)
-        gain_raw = keep.tile([P, NS, H], BF16, name="gain_raw")
-        nc.sync.dma_start(out=gain_raw[:].rearrange("p j h -> p (j h)"),
-                          in_=scale_gain.rearrange("j h -> (j h)").partition_broadcast(P))
-        skip_raw = keep.tile([P, 2], BF16, name="skip_raw")
-        nc.sync.dma_start(out=skip_raw[:], in_=skip_w.partition_broadcast(P))
-        nc.sync.dma_start(out=bk_rows[0:TILES, :].rearrange("t (h i) -> t h i", i=8),
-                          in_=bkv[0:D].rearrange("(h t i) -> t h i", t=TILES, i=8))
-        load_x(0, 2)
-        load_x(0, 3)
-        for q in range(4):
-            nc.sync.dma_start(out=plane[32 * q:32 * q + 4, :, :].bitcast(I32),
-                              in_=Wkv_scales[:, 4 * q:4 * q + 4, :].rearrange("g r n -> r g n").bitcast(I32))
+        for r in range(RC):
+            load_x(0, r)
         wk_raw = work.tile([P, PASSES, 2 * D], U8, name="wk_raw", tag="stage", bufs=3)
         nc.sync.dma_start(out=wk_raw[:].bitcast(I32),
                           in_=Wkv_words[:, :, 0:2 * D].rearrange("g p n -> p g n").bitcast(I32))
         load_x_pair(0, 4)
         load_x_pair(0, 6)
+        gain_raw = keep.tile([P, NS, H], BF16, name="gain_raw")
+        nc.sync.dma_start(out=gain_raw[:].rearrange("p j h -> p (j h)"),
+                          in_=scale_gain.rearrange("j h -> (j h)").partition_broadcast(P))
+        skip_raw = keep.tile([P, 2], BF16, name="skip_raw")
+        nc.sync.dma_start(out=skip_raw[:], in_=skip_w.partition_broadcast(P))
         wv = keep.tile([P, PASSES, 2 * D], U8, name="wv", align_bytes=64)
         nc.sync.dma_start(out=wv[:].bitcast(I32),
                           in_=Wkv_words[:, :, 2 * D:4 * D].rearrange("g p n -> p g n").bitcast(I32))
@@ -128,6 +126,8 @@ def tile_causalwaveletfieldattentionh_pa_kernel(tc, x, Wkv_words, Wkv_scales, bk
             nc.vector.tensor_scalar(out=sw[:], in0=sw[:], scalar1=0.5, scalar2=0.5, op0=ALU.mult, op1=ALU.add)
             nc.vector.reciprocal(out=total[:], in_=total[:])
             nc.vector.tensor_tensor(out=gain[:], in0=gain[:], in1=total[:].unsqueeze(1).to_broadcast([P, NS, H]), op=ALU.mult)
+
+        def coefficient_rows():
             nc.vector.tensor_scalar(out=coef[:, 0:NS, :], in0=gain[:], scalar1=D4[2], scalar2=None, op0=ALU.mult)
             nc.vector.tensor_scalar(out=coef[:, NS, :], in0=gain[:, NS - 1, :], scalar1=D4[1], scalar2=None, op0=ALU.mult)
             nc.vector.tensor_scalar(out=coef[:, NS + 1:, :], in0=gain[:], scalar1=D4[0], scalar2=None, op0=ALU.mult)
@@ -141,18 +141,25 @@ def tile_causalwaveletfieldattentionh_pa_kernel(tc, x, Wkv_words, Wkv_scales, bk
         toep = keep.tile([P, H, 2 * P], F32, name="toep")
 
         def build_filter():
-            nc.gpsimd.tensor_scalar(out=filt[:, :, LEAD], in0=top[:], scalar1=D4[3], scalar2=0.0, op0=ALU.mult, op1=ALU.add)
-            for k in range(3, NS + 1):
-                nc.gpsimd.tensor_copy(out=filt[:, :, LEAD + 2 ** (k - 3)], in_=coef[:, k, :])
-            for j in range(3, NS):
-                nc.gpsimd.tensor_copy(out=filt[:, :, LEAD + 3 * 2 ** (j - 3)], in_=coef[:, NS + 1 + j, :])
+            nc.vector.tensor_scalar(out=filt[:, :, LEAD], in0=top[:], scalar1=D4[3], scalar2=None, op0=ALU.mult)
+            nc.vector.tensor_copy(out=filt[:, :, LEAD + 1], in_=coef[:, 3, :])
+            for k in range(5):
+                nc.vector.tensor_copy(out=filt[:, :, LEAD + 2 * 2 ** k:LEAD + 3 * 2 ** k + 1:2 ** k],
+                               in_=coef[:, k + 4:k + 5 + NS:NS, :].rearrange("p s h -> p h s"))
+            for i in range(2):
+                nc.vector.tensor_scalar(out=filt[:, :, LEAD + 64 * (i + 1):LEAD + 64 * (i + 1) + 49], in0=filt[:, :, LEAD:LEAD + 49],
+                                        scalar1=sw[:, i:i + 1], scalar2=None, op0=ALU.mult)
 
         def skip_filter():
-            used = (slice(0, 49), slice(0, 33, 32), slice(0, 1))
-            for dst, src, i in ((3, 2, 0), (3, 1, 1), (2, 1, 0), (2, 0, 1), (1, 0, 0)):
-                to = filt[:, :, LEAD + 64 * dst:LEAD + 64 * (dst + 1)][:, :, used[src]]
-                nc.vector.scalar_tensor_tensor(out=to, in0=filt[:, :, LEAD + 64 * src:LEAD + 64 * (src + 1)][:, :, used[src]],
-                                               scalar=sw[:, i:i + 1], in1=to, op0=ALU.mult, op1=ALU.add)
+            pair = coef[:, 9:20:NS, :].rearrange("p s h -> p h s")
+            at = [filt[:, :, LEAD + 64 * q:LEAD + 64 * q + 33:32] for q in range(4)]
+            nc.vector.tensor_scalar(out=at[3], in0=pair, scalar1=sw[:, 1:2], scalar2=None, op0=ALU.mult)
+            nc.vector.tensor_tensor(out=at[1], in0=at[1], in1=pair, op=ALU.add)
+            nc.vector.scalar_tensor_tensor(out=at[2], in0=pair, scalar=sw[:, 0:1], in1=at[2], op0=ALU.mult, op1=ALU.add)
+            nc.vector.scalar_tensor_tensor(out=at[3][:, :, 0], in0=coef[:, 10, :], scalar=sw[:, 0:1], in1=at[3][:, :, 0],
+                                           op0=ALU.mult, op1=ALU.add)
+            ends = filt[:, :, LEAD + 128:LEAD + 193:64]
+            nc.vector.tensor_tensor(out=ends, in0=ends, in1=coef[:, 10:21:NS, :].rearrange("p s h -> p h s"), op=ALU.add)
 
         flat = out.rearrange("b h n c -> (b h n c)")
 
@@ -178,7 +185,7 @@ def tile_causalwaveletfieldattentionh_pa_kernel(tc, x, Wkv_words, Wkv_scales, bk
                 for u in range(2):
                     nc.tensor.transpose(ps[:, (2 * g + u) * P:(2 * g + u + 1) * P],
                                         words[:, 256 * g + u:256 * (g + 1):2], ident[:])
-            move = nc.vector.tensor_copy if (c == 1 or (c == 0 and rr % 2 == 1)) else nc.scalar.copy
+            move = nc.vector.tensor_copy if (c in (1, 2) or (c == 0 and rr % 2 == 1)) else nc.scalar.copy
             move(out=grouped[c][:, :, rr, :, :], in_=ps[:].rearrange("k (g u p) -> k g p u", g=PASSES, u=2))
 
         def quantize(c):
@@ -201,12 +208,15 @@ def tile_causalwaveletfieldattentionh_pa_kernel(tc, x, Wkv_words, Wkv_scales, bk
         def add_keys(c, t):
             nc.vector.tensor_tensor(out=ksq[c, t % 2][:], in0=ksq[c, t % 2][:], in1=ksq[c, t][:], op=ALU.add)
 
-        def sum_keys(c, t):
-            if t == 0:
+        def last_keys(c):
+            return [0, 1] + [t for t in (TILES - 2, TILES - 1) if t >= 2 + ADDED[c]]
+
+        def sum_keys(c, t, opens, closes):
+            if opens:
                 ksum[c] = bank()
             for rr in range(RC):
                 nc.tensor.matmul(ksum[c][:, P * rr:P * (rr + 1)], lhsT=ksq[c, t][:, P * rr:P * (rr + 1)], rhs=ident[:],
-                                 is_transpose=True, start=(t == 0 and rr == 0), stop=(t == TILES - 1 and rr == RC - 1))
+                                 is_transpose=True, start=(opens and rr == 0), stop=(closes and rr == RC - 1))
 
         def square_sums(c):
             to = mag[:, c // 2, RC * (c % 2):RC * (c % 2 + 1), :].rearrange("p r h -> p (r h)")
@@ -355,69 +365,79 @@ def tile_causalwaveletfieldattentionh_pa_kernel(tc, x, Wkv_words, Wkv_scales, bk
                 move(out=res[:, :, RC * b:RC * (b + 1), :], in_=ps[b][:].rearrange("p (r e c) -> p e r c", e=2, c=HD))
             nc.sync.dma_start(out=rows, in_=res[:].rearrange("p e r c -> p e (r c)"))
 
-        coefficients()
-        turn_x(0, 0)
-        turn_x(0, 1)
-        turn_x(0, 2)
-        turn_x(0, 3)
+        for rr in range(RC):
+            turn_x(0, rr)
         key_bias()
         order_key_columns()
         quantize(0)
-        coefficients_rest()
-        build_filter()
-        for rr in range(RC):
-            turn_x(1, rr)
-        load_x_pair(1, 2)
         for c in range(2):
             for t in range(TILES):
                 keys(c, t)
                 if c == 0 and t == 0:
+                    coefficients()
+                if c == 0 and t == 2:
+                    for rr in range(RC):
+                        turn_x(1, rr)
+                    load_x_pair(1, 2)
+                    coefficients_rest()
                     quantize(1)
-                if 2 <= t < TILES - 1:
-                    add_keys(c, t)
-                if c == 1 and t == 1:
-                    for tt in (0, 1, TILES - 1):
-                        sum_keys(0, tt)
+                if c == 0 and t == 6:
+                    coefficient_rows()
+                    build_filter()
                     skip_filter()
                     park_filter()
+                if 2 <= t < 2 + ADDED[c]:
+                    add_keys(c, t)
+                if t >= 2 + ADDED[c] + 2:
+                    sum_keys(c, t - 2, t == 2 + ADDED[c] + 2, False)
+                if c == 1 and t == 2:
+                    for tt in last_keys(0):
+                        sum_keys(0, tt, tt == last_keys(0)[0] and ADDED[0] >= 4, tt == last_keys(0)[-1])
                     square_sums(0)
         fetch_filter()
         values(0, 0)
         values(0, 1)
-        for tt in (0, 1, TILES - 1):
-            sum_keys(1, tt)
+        for tt in last_keys(1):
+            sum_keys(1, tt, tt == last_keys(1)[0] and ADDED[1] >= 4, tt == last_keys(1)[-1])
         values(1, 0)
         values(1, 1)
         magnitude(0, 0)
         value_bias(0, 0)
-        square_sums(1)
         value_bias(0, 1)
+        square_sums(1)
         scale_values(0, 0)
+        value_bias(1, 0)
         magnitude(1, 1)
         scale_values(0, 1)
-        value_bias(1, 0)
         value_bias(1, 1)
         scale_values(1, 0)
         scale_values(1, 1)
-        values(2, 0)
-        values(2, 1)
+        turn_x(2, 0)
+        turn_x(2, 1)
+        def key_products(c, t0):
+            return [(keys, c, t) for t in range(t0, t0 + 4)]
+
+        def key_turns(c, t0):
+            return [(sum_keys, c, t, t == 0, t == TILES - 1) for t in range(t0, t0 + 4)]
+
         key_work = [
-            ([], [(turn_x, 2, rr) for rr in range(RC)] + [(load_x_pair, 1, 6)], [(quantize, 2)]),
-            ([(keys, 2, t) for t in range(0, 4)], [(turn_x, 3, 0), (turn_x, 3, 1)], []),
-            ([(keys, 2, t) for t in range(4, 8)], [(sum_keys, 2, t) for t in range(0, 4)] + [(turn_x, 3, 2), (turn_x, 3, 3)], []),
-            ([(keys, 3, t) for t in range(0, 4)], [(sum_keys, 2, t) for t in range(4, 8)], [(quantize, 3), (square_sums, 2), (magnitude, 2, 2)]),
-            ([(keys, 3, t) for t in range(4, 8)], [(sum_keys, 3, t) for t in range(0, 4)], []),
-            ([], [(sum_keys, 3, t) for t in range(4, 8)], [(square_sums, 3), (magnitude, 3, 3)]),
+            (key_products(2, 0), [], []),
+            (key_products(2, 4), key_turns(2, 0), []),
+            ([], key_turns(2, 4) + [(turn_x, 3, rr) for rr in range(RC)], [(square_sums, 2), (magnitude, 2, 2)]),
+            (key_products(3, 0), [], []),
+            (key_products(3, 4), key_turns(3, 0), []),
+            ([], key_turns(3, 4), [(square_sums, 3), (magnitude, 3, 3)]),
         ]
         order = [(a, j) for a in range(HALVES) for j in range(TILES)]
         turn_field(*order[0])
-        for e in range(2):
-            value_bias(2, e)
         add_skips(*order[0])
         start_sums(*order[0])
+        turn_x(2, 2)
+        turn_x(2, 3)
         load_x_pair(1, 4)
-        for e in range(2):
-            scale_values(2, e)
+        load_x_pair(1, 6)
+        values(2, 0)
+        values(2, 1)
         for i, (a, j) in enumerate(order):
             products, turns, after = key_work[i] if i < len(key_work) else ([], [], [])
             more = i + 1 < len(order)
@@ -428,11 +448,20 @@ def tile_causalwaveletfieldattentionh_pa_kernel(tc, x, Wkv_words, Wkv_scales, bk
                 values(u, 0)
                 values(u, 1)
             add_tap(a, j, 0)
+            if i == 0:
+                value_bias(2, 0)
+                value_bias(2, 1)
+                quantize(2)
             if u < 16:
                 value_bias(u, 0)
                 value_bias(u, 1)
             if more:
                 add_skips(*order[i + 1])
+            if i == 3:
+                quantize(3)
+            if i == 0:
+                scale_values(2, 0)
+                scale_values(2, 1)
             if u < 16:
                 scale_values(u, 0)
                 scale_values(u, 1)

from contextlib import ExitStack

import concourse.mybir as mybir
from concourse.masks import make_identity

N, D, H, HD, NS = 2048, 1024, 16, 64, 10
D4 = (0.4829629131445341, 0.8365163037378079, 0.2241438680420134, -0.1294095225512604)
FLOPS = 2 * N * D * 2 * D

F32 = mybir.dt.float32
BF16 = mybir.dt.bfloat16
I32 = mybir.dt.int32
U32 = mybir.dt.uint32
U8 = mybir.dt.uint8
E5M2X4 = mybir.dt.float8_e5m2_x4
E2M1X4 = mybir.dt.float4_e2m1fn_x4
ALU = mybir.AluOpType
ACT = mybir.ActivationFunctionType
AX = mybir.AxisListType

P = 128
R = 8
HALVES = 2
PASSES = 2
RC = 4
TILES = 8
HALO = 4
LEAD = 128
ROW = LEAD + 2 * P
PITCH = H * ROW + 8
EARLY_FROM = 15
ADDED = (4, 4)
CHAINS = ((1, 1, 1, 1, 1, 2, 3, 3), (3, 2, 2, 2, 2, 2, 2, 2))


def tile_causalwaveletfieldattentionh_pa_kernel(tc, x, Wkv_words, Wkv_scales, bkv, scale_gain, skip_w, out):
    nc = tc.nc
    with ExitStack() as ctx:
        keep = ctx.enter_context(tc.tile_pool(name="keep", bufs=1))
        work = ctx.enter_context(tc.tile_pool(name="work", bufs=2))
        psum = ctx.enter_context(tc.psum_pool(name="psum", bufs=1))

        ctx.enter_context(tc.manual_schedule())

        def bank():
            return psum.tile([P, 512], F32, name="bank", tag="bank", bufs=8)

        bk_rows = keep.tile([P, P], BF16, name="bk_rows")
        nc.vector.memset(bk_rows[:], 0.0)
        plane = keep.tile([P, PASSES, 2 * D], U8, name="plane", align_bytes=64)
        nc.vector.memset(plane[:].rearrange("p g n -> p (g n)").bitcast(I32), 0)
        ident = keep.tile([P, P], F32, name="ident")
        make_identity(nc, ident[:])
        filt = keep.tile([P, H, ROW], F32, name="filt", tag="field1")
        nc.vector.memset(filt[:], 0.0)
        nc.scalar.dma_start(out=bk_rows[0:TILES, :].rearrange("t (h i) -> t h i", i=8),
                            in_=bkv[0:D].rearrange("(h t i) -> t h i", t=TILES, i=8))
        for q in range(4):
            nc.scalar.dma_start(out=plane[32 * q:32 * q + 4, :, :].bitcast(I32),
                                in_=Wkv_scales[:, 4 * q:4 * q + 4, :].rearrange("g r n -> r g n").bitcast(I32))

        x_rows = {}

        def load_x(a, r):
            xs = work.tile([P, D], BF16, name="xs", tag="ksq", bufs=7)
            nc.sync.dma_start(out=xs[:], in_=x[0, 1024 * a:1024 * (a + 1), :].rearrange("(p r) k -> p r k", r=R)[:, r, :])
            x_rows[a, r] = xs[:]

        def load_x_pair(a, r):
            xs = work.tile([P, 2, D], BF16, name="xs2", tag="near1", bufs=3)
            nc.sync.dma_start(out=xs[:], in_=x[0, 1024 * a:1024 * (a + 1), :].rearrange("(p r) k -> p r k", r=R)[:, r:r + 2, :])
            x_rows[a, r], x_rows[a, r + 1] = xs[:, 0, :], xs[:, 1, :]

        for r in range(RC):
            load_x(0, r)
        wk_raw = work.tile([P, PASSES, 2 * D], U8, name="wk_raw", tag="stage", bufs=3)
        nc.sync.dma_start(out=wk_raw[:].bitcast(I32),
                          in_=Wkv_words[:, :, 0:2 * D].rearrange("g p n -> p g n").bitcast(I32))
        load_x_pair(0, 4)
        load_x_pair(0, 6)
        gain_raw = keep.tile([P, NS, H], BF16, name="gain_raw")
        nc.sync.dma_start(out=gain_raw[:].rearrange("p j h -> p (j h)"),
                          in_=scale_gain.rearrange("j h -> (j h)").partition_broadcast(P))
        skip_raw = keep.tile([P, 2], BF16, name="skip_raw")
        nc.sync.dma_start(out=skip_raw[:], in_=skip_w.partition_broadcast(P))
        wv = keep.tile([P, PASSES, 2 * D], U8, name="wv", align_bytes=64)
        nc.sync.dma_start(out=wv[:].bitcast(I32),
                          in_=Wkv_words[:, :, 2 * D:4 * D].rearrange("g p n -> p g n").bitcast(I32))
        bv = keep.tile([P, D], BF16, name="bv")
        nc.sync.dma_start(out=bv[:], in_=bkv[D:2 * D].partition_broadcast(P))
        load_x_pair(1, 0)

        wk = keep.tile([P, PASSES, 2 * D], U8, name="wk", align_bytes=64)
        sk = keep.tile([P, PASSES, D], U8, name="sk", align_bytes=64)
        bk_f32 = keep.tile([P, P], F32, name="bk_f32")
        bk = keep.tile([P, TILES], F32, name="bk")
        top = keep.tile([P, H], F32, name="top")
        gain = keep.tile([P, NS, H], F32, name="gain")
        sw = keep.tile([P, 2], F32, name="sw")
        total = keep.tile([P, H], F32, name="total")
        coef = keep.tile([P, 2 * NS + 1, H], F32, name="coef")
        coef_ch = keep.tile([P, 2 * NS + 1, TILES], F32, name="coef_ch")
        def order_key_columns():
            for g in range(PASSES):
                nc.vector.tensor_copy(out=sk[:, g, :].bitcast(I32).rearrange("p (t h w) -> p t h w", t=TILES, h=H),
                                      in_=plane[:, g, 0:D].bitcast(I32).rearrange("p (h t w) -> p t h w", t=TILES, h=H))
            for g in range(PASSES):
                nc.scalar.copy(out=wk[:, g, :].bitcast(U32).rearrange("p (t h w) -> p t h w", t=TILES, h=H),
                               in_=wk_raw[:, g, :].bitcast(U32).rearrange("p (h t w) -> p t h w", t=TILES, h=H))

        nc.vector.tensor_copy(out=bk_f32[:], in_=bk_rows[:])

        def key_bias():
            bk_ps = bank()
            nc.tensor.transpose(bk_ps[:, 0:P], bk_f32[:], ident[:])
            nc.vector.tensor_copy(out=bk[:], in_=bk_ps[:, 0:TILES])

        def coefficients():
            nc.vector.tensor_reduce(out=top[:], in_=gain_raw[:].rearrange("p j h -> p h j"), axis=AX.X, op=ALU.max)
            nc.vector.tensor_tensor(out=gain[:], in0=gain_raw[:], in1=top[:].unsqueeze(1).to_broadcast([P, NS, H]), op=ALU.subtract)

        def coefficients_rest():
            nc.scalar.activation(out=gain[:], in_=gain[:], func=ACT.Exp)
            nc.scalar.activation(out=sw[:], in_=skip_raw[:], func=ACT.Tanh, scale=0.5)
            nc.vector.tensor_reduce(out=total[:], in_=gain[:].rearrange("p j h -> p h j"), axis=AX.X, op=ALU.add)
            nc.vector.tensor_scalar(out=sw[:], in0=sw[:], scalar1=0.5, scalar2=0.5, op0=ALU.mult, op1=ALU.add)
            nc.vector.reciprocal(out=total[:], in_=total[:])
            nc.vector.tensor_tensor(out=gain[:], in0=gain[:], in1=total[:].unsqueeze(1).to_broadcast([P, NS, H]), op=ALU.mult)

        def coefficient_rows():
            nc.vector.tensor_scalar(out=coef[:, 0:NS, :], in0=gain[:], scalar1=D4[2], scalar2=None, op0=ALU.mult)
            nc.vector.tensor_scalar(out=coef[:, NS, :], in0=gain[:, NS - 1, :], scalar1=D4[1], scalar2=None, op0=ALU.mult)
            nc.vector.tensor_scalar(out=coef[:, NS + 1:, :], in0=gain[:], scalar1=D4[0], scalar2=None, op0=ALU.mult)
            nc.vector.scalar_tensor_tensor(out=coef[:, 1:NS, :], in0=gain[:, 0:NS - 1, :], scalar=D4[1], in1=coef[:, 1:NS, :],
                                           op0=ALU.mult, op1=ALU.add)
            nc.vector.tensor_reduce(out=top[:], in_=gain[:].rearrange("p j h -> p h j"), axis=AX.X, op=ALU.add)
            for hh in range(2):
                rows = slice(HD * hh, HD * (hh + 1))
                nc.vector.tensor_copy(out=coef_ch[rows], in_=coef[rows].rearrange("p s (j e) -> p s j e", e=2)[:, :, :, hh])

        toep = keep.tile([P, H, 2 * P], F32, name="toep")

        def build_filter():
            nc.vector.tensor_scalar(out=filt[:, :, LEAD], in0=top[:], scalar1=D4[3], scalar2=None, op0=ALU.mult)
            nc.vector.tensor_copy(out=filt[:, :, LEAD + 1], in_=coef[:, 3, :])
            for k in range(5):
                nc.vector.tensor_copy(out=filt[:, :, LEAD + 2 * 2 ** k:LEAD + 3 * 2 ** k + 1:2 ** k],
                               in_=coef[:, k + 4:k + 5 + NS:NS, :].rearrange("p s h -> p h s"))
            for i in range(2):
                nc.vector.tensor_scalar(out=filt[:, :, LEAD + 64 * (i + 1):LEAD + 64 * (i + 1) + 49], in0=filt[:, :, LEAD:LEAD + 49],
                                        scalar1=sw[:, i:i + 1], scalar2=None, op0=ALU.mult)

        def skip_filter():
            pair = coef[:, 9:20:NS, :].rearrange("p s h -> p h s")
            at = [filt[:, :, LEAD + 64 * q:LEAD + 64 * q + 33:32] for q in range(4)]
            nc.vector.tensor_scalar(out=at[3], in0=pair, scalar1=sw[:, 1:2], scalar2=None, op0=ALU.mult)
            nc.vector.tensor_tensor(out=at[1], in0=at[1], in1=pair, op=ALU.add)
            nc.vector.scalar_tensor_tensor(out=at[2], in0=pair, scalar=sw[:, 0:1], in1=at[2], op0=ALU.mult, op1=ALU.add)
            nc.vector.scalar_tensor_tensor(out=at[3][:, :, 0], in0=coef[:, 10, :], scalar=sw[:, 0:1], in1=at[3][:, :, 0],
                                           op0=ALU.mult, op1=ALU.add)
            ends = filt[:, :, LEAD + 128:LEAD + 193:64]
            nc.vector.tensor_tensor(out=ends, in0=ends, in1=coef[:, 10:21:NS, :].rearrange("p s h -> p h s"), op=ALU.add)

        flat = out.rearrange("b h n c -> (b h n c)")

        def park_filter():
            nc.sync.dma_start(out=flat[0:P * PITCH].rearrange("(p w) -> p w", w=PITCH)[:, 0:H * ROW],
                              in_=filt[:].rearrange("p h w -> p (h w)"))

        def fetch_filter():
            skew = flat[0:P * (PITCH - 1)].rearrange("(p w) -> p w", w=PITCH - 1)[:, 0:H * ROW]
            nc.sync.dma_start(out=toep[:], in_=skew.rearrange("p (h w) -> p h w", w=ROW)[:, :, LEAD:])

        field = {}
        mag = keep.tile([P, HALVES, R, H], F32, name="mag")
        grouped, codes, scales, ksq, ksum = {}, {}, {}, {}, {}

        def turn_x(c, rr):
            a, r = c // 2, RC * (c % 2) + rr
            if rr == 0:
                grouped[c] = work.tile([P, PASSES, RC, P, 2], F32, name="grouped", tag="grouped", align_bytes=64)
            words = x_rows[a, r].bitcast(F32)
            ps = bank()
            for g in range(PASSES):
                for u in range(2):
                    nc.tensor.transpose(ps[:, (2 * g + u) * P:(2 * g + u + 1) * P],
                                        words[:, 256 * g + u:256 * (g + 1):2], ident[:])
            move = nc.vector.tensor_copy if (c in (1, 2) or (c == 0 and rr % 2 == 1)) else nc.scalar.copy
            move(out=grouped[c][:, :, rr, :, :], in_=ps[:].rearrange("k (g u p) -> k g p u", g=PASSES, u=2))

        def quantize(c):
            codes[c] = work.tile([P, PASSES, RC * P], U32, name="codes", tag="codes", bufs=3, align_bytes=64)
            scales[c] = work.tile([P, PASSES, RC * P], U8, name="scales", tag="scales", bufs=3, align_bytes=64)
            for g in range(PASSES):
                nc.vector.quantize_mx(out=codes[c][:, g, :].bitcast(E5M2X4), scales=scales[c][:, g, :],
                                      in_=grouped[c][:, g].rearrange("k r p u -> k (r p u)").bitcast(BF16))

        def keys(c, t):
            ps = bank()
            for g in range(PASSES):
                nc.tensor.matmul_mx(out=ps[:], lhsT=wk[:, g, 2 * P * t:2 * P * (t + 1)].bitcast(E2M1X4),
                                    lhsT_scale=sk[:, g, P * t:P * (t + 1)],
                                    rhs=codes[c][:, g, :].bitcast(E5M2X4), rhs_scale=scales[c][:, g, :],
                                    start=(g == 0), stop=(g == PASSES - 1))
            ksq[c, t] = work.tile([P, RC * P], F32, name="ksq", tag="ksq", bufs=7)
            nc.scalar.activation(out=ksq[c, t][:], in_=ps[:], func=ACT.Square, bias=bk[:, t:t + 1])

        def add_keys(c, t):
            nc.vector.tensor_tensor(out=ksq[c, t % 2][:], in0=ksq[c, t % 2][:], in1=ksq[c, t][:], op=ALU.add)

        def last_keys(c):
            return [0, 1] + [t for t in (TILES - 2, TILES - 1) if t >= 2 + ADDED[c]]

        def sum_keys(c, t, opens, closes):
            if opens:
                ksum[c] = bank()
            for rr in range(RC):
                nc.tensor.matmul(ksum[c][:, P * rr:P * (rr + 1)], lhsT=ksq[c, t][:, P * rr:P * (rr + 1)], rhs=ident[:],
                                 is_transpose=True, start=(opens and rr == 0), stop=(closes and rr == RC - 1))

        def square_sums(c):
            to = mag[:, c // 2, RC * (c % 2):RC * (c % 2 + 1), :].rearrange("p r h -> p (r h)")
            nc.vector.tensor_reduce(out=to, in_=ksum[c][:].rearrange("p (e i) -> p e i", i=8), axis=AX.X, op=ALU.add)

        def magnitude(c0, c1):
            to = mag[:].rearrange("p a r h -> p (a r h)")[:, RC * H * c0:RC * H * (c1 + 1)]
            nc.scalar.activation(out=to, in_=to, func=ACT.Sqrt)

        raw_values = {}

        def unit_view(u):
            a, q, b = u // 8, u // 2 % 4, u % 2
            if a not in field:
                field[a] = keep.tile([P, R, D], F32, name="field", tag="field%d" % a)
            return a, q, b

        def values(u, e):
            a, q, b = unit_view(u)
            c = 2 * a + b
            ps = raw_values[u, e] = bank()
            for rr in (2 * e, 2 * e + 1):
                for g in range(PASSES):
                    nc.tensor.matmul_mx(out=ps[:, 256 * (rr % 2):256 * (rr % 2 + 1)],
                                        lhsT=codes[c][:, g, P * rr:P * (rr + 1)].bitcast(E5M2X4),
                                        lhsT_scale=scales[c][:, g, P * rr:P * (rr + 1)],
                                        rhs=wv[:, g, 512 * q:512 * (q + 1)].bitcast(E2M1X4),
                                        rhs_scale=plane[:, g, D + 256 * q:D + 256 * (q + 1)],
                                        start=(g == 0), stop=(g == PASSES - 1))

        def value_bias(u, e):
            a, q, b = unit_view(u)
            r0, cols = RC * b + 2 * e, slice(256 * q, 256 * (q + 1))
            nc.vector.tensor_tensor(out=field[a][:, r0:r0 + 2, cols], in0=raw_values[u, e][:].rearrange("p (r c) -> p r c", r=2),
                                    in1=bv[:, cols].unsqueeze(1).to_broadcast([P, 2, 256]), op=ALU.add)

        def scale_values(u, e):
            a, q, b = unit_view(u)
            r0 = RC * b + 2 * e
            if u == 1 and e == 1:
                v = field[a][:, r0:r0 + 2, 256 * q:256 * (q + 1)].rearrange("p r (h c) -> p r h c", c=HD)
                nc.vector.tensor_tensor(out=v, in0=v, op=ALU.mult,
                                        in1=mag[:, a, r0:r0 + 2, 4 * q:4 * q + 4].unsqueeze(3).to_broadcast([P, 2, 4, HD]))
            else:
                for r in (r0, r0 + 1):
                    for h in range(4 * q, 4 * q + 4):
                        v = field[a][:, r, HD * h:HD * (h + 1)]
                        nc.scalar.activation(out=v, in_=v, func=ACT.Copy, scale=mag[:, a, r, h:h + 1])

        def run(calls):
            for call in calls:
                call[0](*call[1:])

        first = keep.tile([P, TILES, R, HALO + P], F32, name="first")
        second_raw = keep.tile([P, TILES, R, 64], F32, name="second_raw")
        nc.vector.memset(first[:, :, :, 0:HALO].rearrange("p j r w -> p (j r) w"), 0.0)
        skipped, sums = {}, {}

        turned = {}

        def turn_field(a, j):
            ps = [bank(), bank()]
            for r in range(R):
                nc.tensor.transpose(ps[r // RC][:, P * (r % RC):P * (r % RC + 1)], field[a][:, r, P * j:P * (j + 1)], ident[:])
            turned[a, j] = [b[:].rearrange("c (r p) -> c r p", p=P) for b in ps]

        def add_skips(a, j):
            views = turned[a, j]
            q0 = first[:, j, :, HALO:HALO + 64]
            q1 = second_raw[:, j]
            if a == 0:
                for b in range(2):
                    rs = slice(RC * b, RC * (b + 1))
                    nc.scalar.copy(out=q0[:, rs, :], in_=views[b][:, :, 0:64])
                    nc.scalar.copy(out=q1[:, rs, :], in_=views[b][:, :, 64:P])
                nc.vector.scalar_tensor_tensor(out=first[:, j, :, HALO + 64:], in0=q0, scalar=sw[:, 0:1], in1=q1,
                                               op0=ALU.mult, op1=ALU.add)
                skipped[a, j] = first[:, j]
            else:
                later = work.tile([P, R, HALO + P], F32, name="later", tag="grouped", align_bytes=64)
                lo, hi = later[:, :, HALO:HALO + 64], later[:, :, HALO + 64:]
                nc.scalar.copy(out=later[:, :, 0:HALO], in_=first[:, j, :, P:P + HALO])
                for b in range(2):
                    rs = slice(RC * b, RC * (b + 1))
                    nc.vector.scalar_tensor_tensor(out=hi[:, rs, :], in0=q1[:, rs, :], scalar=sw[:, 1:2], in1=views[b][:, :, 64:P],
                                                   op0=ALU.mult, op1=ALU.add)
                    nc.vector.scalar_tensor_tensor(out=lo[:, rs, :], in0=q1[:, rs, :], scalar=sw[:, 0:1], in1=views[b][:, :, 0:64],
                                                   op0=ALU.mult, op1=ALU.add)
                for b in range(2):
                    rs = slice(RC * b, RC * (b + 1))
                    nc.vector.scalar_tensor_tensor(out=hi[:, rs, :], in0=views[b][:, :, 0:64], scalar=sw[:, 0:1], in1=hi[:, rs, :],
                                                   op0=ALU.mult, op1=ALU.add)
                nc.vector.scalar_tensor_tensor(out=lo, in0=q0, scalar=sw[:, 1:2], in1=lo, op0=ALU.mult, op1=ALU.add)
                skipped[a, j] = later[:]

        def tap_pieces(src, dst, shift):
            whole, w = divmod(shift, R)
            return ((dst[:, w:R, :], src[:, 0:R - w, HALO - whole:HALO - whole + P]),
                    (dst[:, 0:w, :], src[:, R - w:R, HALO - whole - 1:HALO - whole - 1 + P]))

        COEF_ROW = {1: 0, 2: 1, 4: 2, 3: NS + 1, 6: NS + 2, 12: NS + 3}

        def start_sums(a, j):
            starts = (1, 12, 6)[:CHAINS[a][j]]
            sums[a, j] = []
            for e, shift in enumerate(starts):
                s = work.tile([P, R, P], F32, name="near", tag=("near0", "near1", "stage")[e], bufs=3)
                for to, src in tap_pieces(skipped[a, j], s, shift):
                    nc.scalar.activation(out=to, in_=src, func=ACT.Copy, scale=coef_ch[:, COEF_ROW[shift], j:j + 1])
                sums[a, j].append(s)

        def add_tap(a, j, e):
            for shift in ((2, 3, 4, 12, 6), (2, 3, 4, 6), (2, 3, 4))[CHAINS[a][j] - 1][e:e + 1]:
                for to, src in tap_pieces(skipped[a, j], sums[a, j][0], shift):
                    nc.vector.scalar_tensor_tensor(out=to, in0=src, scalar=coef_ch[:, COEF_ROW[shift], j:j + 1], in1=to,
                                                   op0=ALU.mult, op1=ALU.add)

        acc = {}

        def far_taps(a, j):
            ps = acc[a, j] = [bank(), bank()]
            for hh in range(2):
                h = 2 * j + hh
                for back in range(a + 1):
                    for b in range(2):
                        nc.tensor.matmul(ps[b][:].rearrange("p (r e c) -> p r e c", e=2, c=HD)[:, :, hh, :],
                                         lhsT=toep[:, h, P * back:P * (back + 1)],
                                         rhs=field[a - back][:, RC * b:RC * (b + 1), HD * h:HD * (h + 1)],
                                         start=(hh == 0 and back == 0), stop=False)

        def finish(a, j):
            ps = acc[a, j]
            last = len(sums[a, j]) - 1
            for e, s in enumerate(reversed(sums[a, j])):
                for r in range(R):
                    nc.tensor.matmul(ps[r // RC][:, P * (r % RC):P * (r % RC + 1)], lhsT=s[:, r, :], rhs=ident[:],
                                     is_transpose=True, start=False, stop=(e == last and r % RC == RC - 1))

        def store(a, j):
            ps = acc[a, j]
            res = work.tile([P, 2, R, HD], F32, name="res", tag="stage", bufs=3)
            rows = out[0, 2 * j:2 * j + 2, 1024 * a:1024 * (a + 1), :].rearrange("h (p r) c -> p h (r c)", r=R)
            final = (a, j) == (HALVES - 1, TILES - 1)
            for b in range(2):
                move = nc.vector.tensor_copy if final and b == 1 else nc.scalar.copy
                move(out=res[:, :, RC * b:RC * (b + 1), :], in_=ps[b][:].rearrange("p (r e c) -> p e r c", e=2, c=HD))
            nc.sync.dma_start(out=rows, in_=res[:].rearrange("p e r c -> p e (r c)"))

        for rr in range(RC):
            turn_x(0, rr)
        key_bias()
        order_key_columns()
        quantize(0)
        for c in range(2):
            for t in range(TILES):
                keys(c, t)
                if c == 0 and t == 0:
                    coefficients()
                if c == 0 and t == 2:
                    for rr in range(RC):
                        turn_x(1, rr)
                    load_x_pair(1, 2)
                    coefficients_rest()
                    quantize(1)
                if c == 0 and t == 6:
                    coefficient_rows()
                    build_filter()
                    skip_filter()
                    park_filter()
                if 2 <= t < 2 + ADDED[c]:
                    add_keys(c, t)
                if t >= 2 + ADDED[c] + 2:
                    sum_keys(c, t - 2, t == 2 + ADDED[c] + 2, False)
                if c == 1 and t == 2:
                    for tt in last_keys(0):
                        sum_keys(0, tt, tt == last_keys(0)[0] and ADDED[0] >= 4, tt == last_keys(0)[-1])
                    square_sums(0)
        fetch_filter()
        values(0, 0)
        values(0, 1)
        for tt in last_keys(1):
            sum_keys(1, tt, tt == last_keys(1)[0] and ADDED[1] >= 4, tt == last_keys(1)[-1])
        values(1, 0)
        values(1, 1)
        magnitude(0, 0)
        value_bias(0, 0)
        value_bias(0, 1)
        square_sums(1)
        scale_values(0, 0)
        value_bias(1, 0)
        magnitude(1, 1)
        scale_values(0, 1)
        value_bias(1, 1)
        scale_values(1, 0)
        scale_values(1, 1)
        turn_x(2, 0)
        turn_x(2, 1)
        def key_products(c, t0):
            return [(keys, c, t) for t in range(t0, t0 + 4)]

        def key_turns(c, t0):
            return [(sum_keys, c, t, t == 0, t == TILES - 1) for t in range(t0, t0 + 4)]

        key_work = [
            (key_products(2, 0), [], []),
            (key_products(2, 4), key_turns(2, 0), []),
            ([], key_turns(2, 4) + [(turn_x, 3, rr) for rr in range(RC)], [(square_sums, 2), (magnitude, 2, 2)]),
            (key_products(3, 0), [], []),
            (key_products(3, 4), key_turns(3, 0), []),
            ([], key_turns(3, 4), [(square_sums, 3), (magnitude, 3, 3)]),
        ]
        order = [(a, j) for a in range(HALVES) for j in range(TILES)]
        turn_field(*order[0])
        add_skips(*order[0])
        start_sums(*order[0])
        turn_x(2, 2)
        turn_x(2, 3)
        load_x_pair(1, 4)
        load_x_pair(1, 6)
        values(2, 0)
        values(2, 1)
        for i, (a, j) in enumerate(order):
            products, turns, after = key_work[i] if i < len(key_work) else ([], [], [])
            more = i + 1 < len(order)
            u = i + 3
            if more:
                turn_field(*order[i + 1])
            if u < 16:
                values(u, 0)
                values(u, 1)
            add_tap(a, j, 0)
            if i == 0:
                value_bias(2, 0)
                value_bias(2, 1)
                quantize(2)
            if u < 16:
                value_bias(u, 0)
                value_bias(u, 1)
            if more:
                add_skips(*order[i + 1])
            if i == 3:
                quantize(3)
            if i == 0:
                scale_values(2, 0)
                scale_values(2, 1)
            if u < 16:
                scale_values(u, 0)
                scale_values(u, 1)
            if more:
                start_sums(*order[i + 1])
            if 0 < i <= EARLY_FROM:
                far_taps(*order[i - 1])
            if i > 0:
                finish(*order[i - 1])
                store(*order[i - 1])
            if i >= EARLY_FROM:
                far_taps(a, j)
            add_tap(a, j, 1)
            run(turns)
            add_tap(a, j, 2)
            run(after)
            run(products)
            add_tap(a, j, 3)
            add_tap(a, j, 4)
        finish(*order[-1])
        store(*order[-1])
